import numpy as np
import ml_dtypes


def mxq(x, axis, fmt="e4m3"):
    dtype, down = {"e4m3": (ml_dtypes.float8_e4m3fn, 7), "e5m2": (ml_dtypes.float8_e5m2, 14)}[fmt]
    v = np.moveaxis(np.asarray(x, np.float32).astype(ml_dtypes.bfloat16).astype(np.float64), axis, -1)
    blocks = v.reshape(v.shape[:-1] + (-1, 32))
    amax = np.abs(blocks).max(-1, keepdims=True)
    byte = np.maximum(np.where(amax > 0, np.frexp(amax)[1] - 1 + 127, 0) - down, 1)
    scale = np.exp2(byte - 127.0)
    codes = (blocks / scale).astype(np.float32).astype(dtype).astype(np.float64)
    return np.moveaxis((codes * scale).reshape(v.shape), -1, axis)


WIDE = False


def mx_kscale(k):
    if not WIDE:
        return np.ones(k)
    levels = np.array([10, -10, 5, -5, 0])
    a = np.random.permutation(np.resize(levels, k // 512 * 4)).reshape(k // 512, 4)
    idx = np.arange(k)
    return np.exp2(a[idx // 512, idx % 128 // 32])


BF16 = ml_dtypes.bfloat16


def bf(x):
    return np.asarray(x, np.float32).astype(BF16)


def f64(x):
    return np.asarray(x).astype(np.float64)


E2M1 = np.array([0.0, 0.5, 1.0, 1.5, 2.0, 3.0, 4.0, 6.0, -0.0, -0.5, -1.0, -1.5, -2.0, -3.0, -4.0, -6.0])


def pack_weight(w, fmt):
    k, n = w.shape
    w = f64(bf(w)).reshape(k // 32, 32, n)
    amax = np.abs(w).max(1)
    if fmt == "e4m3":
        byte = np.frexp(amax)[1] - 1 + 127 - 7
    else:
        mant, ex = np.frexp(amax / 6.0)
        byte = np.where(mant > 0.5, ex, ex - 1) + 127
    byte = np.clip(np.where(amax > 0, byte, 1), 1, 254)
    scaled = (w * np.exp2(127.0 - byte)[:, None, :]).reshape(k, n).astype(np.float32)
    by_word = np.ascontiguousarray(scaled.reshape(k // 512, 128, 4, n).transpose(0, 1, 3, 2))
    if fmt == "e4m3":
        words = by_word.astype(ml_dtypes.float8_e4m3fn).view(np.uint8)
    else:
        c = by_word.astype(ml_dtypes.float4_e2m1fn).view(np.uint8) & 0xF
        words = c[..., 0::2] | (c[..., 1::2] << 4)
    return np.ascontiguousarray(words), np.ascontiguousarray(byte.astype(np.uint8).reshape(k // 512, 16, n))


def unpack_weight(words, scales, fmt):
    g, p, n, _ = words.shape
    if fmt == "e4m3":
        vals = np.ascontiguousarray(words).view(ml_dtypes.float8_e4m3fn).astype(np.float64)
    else:
        nib = np.empty((g, p, n, 4), np.uint8)
        nib[..., 0::2] = words & 0xF
        nib[..., 1::2] = words >> 4
        vals = E2M1[nib]
    vals = vals * np.repeat(np.exp2(scales.astype(np.float64) - 127.0), 8, axis=1)[..., None]
    return vals.transpose(0, 1, 3, 2).reshape(g * 512, n)

def pack4(w):
    words, scales = pack_weight(w, "e2m1")
    return words.reshape(words.shape[0], 128, -1), scales


def unpack4(words, scales):
    return unpack_weight(words.reshape(words.shape[0], 128, -1, 2), scales, "e2m1")


B, H, L, E, QD = 16, 1, 128, 2048, 128
EPS = 1e-5


def build_decay_mask(num_heads, max_len):
    r = f64(np.arange(max_len))
    dec = np.array([1.0 - 2.0 ** (-5 - h) for h in range(num_heads)])
    expo = r[None, :] - r[:, None]
    return np.where(r[:, None] >= r[None, :], dec[:, None, None] ** expo[None], 0.0)


def setup_inputs():
    s = mx_kscale(E)
    kv = (0.1 + 0.32 * np.random.standard_normal((B, H, L, QD))) * (0.1 + 0.32 * np.random.standard_normal((B, H, L, QD)))
    x = bf(np.random.standard_normal((B, H, L, E)) * s)
    Wq = np.random.standard_normal((QD, E)) / np.sqrt(E) / s
    Wq_words, Wq_scales = pack4(np.ascontiguousarray(Wq.T))
    return {"x": x,
            "Wq_words": Wq_words,
            "Wq_scales": Wq_scales,
            "bq": bf(0.3 + 0.3 * np.random.standard_normal(QD)),
            "kv": bf(kv),
            "decay_mask": bf(build_decay_mask(H, L))}


def reference(x, Wq_words, Wq_scales, bq, kv, decay_mask):
    b, h, l, e = x.shape
    Q = (mxq(f64(x), 3, "e4m3") @ unpack4(Wq_words, Wq_scales)) + f64(bq)
    D = f64(decay_mask)[0, :l, :l]
    y = Q * (f64(kv) @ D.T)
    mean = y.mean(axis=(2, 3), keepdims=True)
    var = ((y - mean) ** 2).mean(axis=(2, 3), keepdims=True)
    y = (y - mean) / np.sqrt(var + EPS)
    return y.reshape(b, l, -1)

@@ -1,0 +1,278 @@
+from contextlib import ExitStack
+
+import concourse.mybir as mybir
+from concourse.masks import make_identity
+
+F32 = mybir.dt.float32
+BF16 = mybir.dt.bfloat16
+I32 = mybir.dt.int32
+U32 = mybir.dt.uint32
+U8 = mybir.dt.uint8
+FP8X4 = mybir.dt.float8_e4m3fn_x4
+FP4X4 = mybir.dt.float4_e2m1fn_x4
+ALU = mybir.AluOpType
+ACT = mybir.ActivationFunctionType
+
+SAMPLES = 16
+L = 128
+E = 2048
+QD = 128
+EPS = 1e-5
+
+P = 128
+PACK = 4
+K_PASS = P * PACK
+PASSES = E // K_PASS
+PAIRS = 2
+BANK_F32 = 512
+TURNS_PER_BANK = BANK_F32 // L
+PASSES_PER_BANK = TURNS_PER_BANK // PAIRS
+BANKS_PER_SAMPLE = PASSES // PASSES_PER_BANK
+ROUND = 2
+ROUNDS = SAMPLES // ROUND
+SCALE_ROWS = 4
+QUADRANTS = 4
+SUM_SLOT = 8
+
+FLOPS = 2 * SAMPLES * L * E * QD + 2 * SAMPLES * L * QD * QD
+
+
+def tile_parallelretention_pb_kernel(tc, x, Wq_words, Wq_scales, bq, kv, decay_mask, out):
+    nc = tc.nc
+    with ExitStack() as ctx:
+        const = ctx.enter_context(tc.tile_pool(name="const", bufs=1))
+        x_pool = ctx.enter_context(tc.tile_pool(name="x", bufs=SAMPLES * BANKS_PER_SAMPLE))
+        kv_pool = ctx.enter_context(tc.tile_pool(name="kv", bufs=ROUNDS))
+        mx_pool = ctx.enter_context(tc.tile_pool(name="mx", bufs=2 * ROUND))
+        work = ctx.enter_context(tc.tile_pool(name="work", bufs=4))
+        res_pool = ctx.enter_context(tc.tile_pool(name="res", bufs=ROUNDS))
+        psum_turn = ctx.enter_context(tc.psum_pool(name="psum_turn", bufs=4))
+        psum_qg = ctx.enter_context(tc.psum_pool(name="psum_qg", bufs=2))
+        psum_small = ctx.enter_context(tc.psum_pool(name="psum_small", bufs=1))
+        ctx.enter_context(tc.manual_schedule())
+
+        ident_f32 = const.tile([P, P], F32)
+        make_identity(nc, ident_f32[:])
+        ident_bf16 = const.tile([P, P], BF16)
+        make_identity(nc, ident_bf16[:])
+        mean_weights = const.tile([P, P], F32)
+        nc.vector.memset(mean_weights[:], 1.0 / (L * QD))
+        w_scales = const.tile([P, PASSES, QD], U8, align_bytes=64)
+        nc.vector.memset(w_scales[:].bitcast(I32), 0)
+
+        table_seed = const.tile([P, 1], F32)
+        nc.vector.memset(table_seed[:], 1.0)
+        nc.scalar.activation(out=table_seed[:], in_=table_seed[:], func=ACT.Abs_reciprocal_sqrt)
+
+        x_rows = {}
+        kv_rows = {}
+
+        def load_x(s):
+            for b in range(BANKS_PER_SAMPLE):
+                x_piece = x_pool.tile([L, E // BANKS_PER_SAMPLE], BF16)
+                nc.sync.dma_start(
+                    out=x_piece[:], in_=x[s, 0, :, b * (E // BANKS_PER_SAMPLE) : (b + 1) * (E // BANKS_PER_SAMPLE)]
+                )
+                x_rows[(s, b)] = x_piece
+
+        def load_kv(r):
+            kv_round = kv_pool.tile([L, ROUND, QD], BF16)
+            nc.sync.dma_start(
+                out=kv_round[:], in_=kv[r * ROUND : (r + 1) * ROUND, 0, :, :].rearrange("s l k -> l s k")
+            )
+            kv_rows[r] = kv_round
+
+        decay_rows = const.tile([QD, QD], BF16)
+        nc.sync.dma_start(out=decay_rows[:], in_=decay_mask[0, :, :])
+        for j in range(ROUND):
+            load_x(j)
+        w_words = const.tile([P, PASSES, 2 * QD], U8, align_bytes=64)
+        nc.sync.dma_start(out=w_words[:].bitcast(I32), in_=Wq_words.bitcast(I32).rearrange("g p w -> p g w"))
+        for quad in range(QUADRANTS):
+            nc.sync.dma_start(
+                out=w_scales[32 * quad : 32 * quad + SCALE_ROWS, :, :].bitcast(I32),
+                in_=Wq_scales.bitcast(I32)[:, SCALE_ROWS * quad : SCALE_ROWS * (quad + 1), :].rearrange(
+                    "g r w -> r g w"
+                ),
+            )
+        load_kv(0)
+        bias_rows = const.tile([P, QD], BF16)
+        nc.sync.dma_start(out=bias_rows[:], in_=bq.partition_broadcast(P))
+        for r in range(1, ROUNDS):
+            for j in range(ROUND):
+                load_x(r * ROUND + j)
+            load_kv(r)
+
+        codes = {}
+        planes = {}
+        kv_turned = {}
+        banks = {}
+        products = {}
+        sums = {}
+        moments = {}
+        means = {}
+        spreads = {}
+        inverses = {}
+
+        def turn_x(r, j):
+            grouped = mx_pool.tile([P, PASSES * L * PACK], BF16, align_bytes=64)
+            grouped_words = grouped[:].bitcast(F32)
+            for b in range(BANKS_PER_SAMPLE):
+                x_words = x_rows[(r * ROUND + j, b)][:].bitcast(F32)
+                turned = psum_turn.tile([P, TURNS_PER_BANK, L], F32)
+                for i in range(PASSES_PER_BANK):
+                    first = i * (K_PASS // 2)
+                    for u in range(PAIRS):
+                        nc.tensor.transpose(
+                            turned[:, i * PAIRS + u, :],
+                            x_words[:, first + u : first + K_PASS // 2 : PAIRS],
+                            ident_f32[:],
+                        )
+                nc.scalar.copy(
+                    out=grouped_words[:, b * BANK_F32 : (b + 1) * BANK_F32].rearrange(
+                        "p (i l u) -> p i l u", i=PASSES_PER_BANK, u=PAIRS
+                    ),
+                    in_=turned[:].rearrange("p (i u) l -> p i l u", u=PAIRS),
+                )
+            return grouped
+
+        def quantise(r, j, grouped):
+            x_codes = mx_pool.tile([P, PASSES * L], U32, align_bytes=64)
+            x_scales = mx_pool.tile([P, PASSES * L], U8, align_bytes=64)
+            nc.vector.quantize_mx(out=x_codes[:].bitcast(FP8X4), scales=x_scales[:], in_=grouped[:])
+            codes[(r, j)] = x_codes
+            planes[(r, j)] = x_scales
+
+        def turn_kv(r):
+            kv_bank = psum_small.tile([QD, ROUND, L], BF16)
+            for j in range(ROUND):
+                nc.tensor.transpose(kv_bank[:, j, :], kv_rows[r][:, j, :], ident_bf16[:])
+            kv_cols = work.tile([QD, ROUND, L], BF16)
+            nc.vector.tensor_copy(out=kv_cols[:], in_=kv_bank[:])
+            kv_turned[r] = kv_cols
+
+        def multiply(r):
+            qg = psum_qg.tile([L, 2 * ROUND, QD], F32)
+            for j in range(ROUND):
+                nc.tensor.matmul(
+                    out=qg[:, ROUND + j, :], lhsT=kv_turned[r][:, j, :], rhs=decay_turned[:], start=True, stop=True
+                )
+            for j in range(ROUND):
+                for g in range(PASSES):
+                    rows = slice(g * L, (g + 1) * L)
+                    nc.tensor.matmul_mx(
+                        out=qg[:, j, :],
+                        lhsT=codes[(r, j)][:, rows].bitcast(FP8X4),
+                        lhsT_scale=planes[(r, j)][:, rows],
+                        rhs=w_words[:, g, :].bitcast(FP4X4),
+                        rhs_scale=w_scales[:, g, :],
+                        start=(g == 0),
+                        stop=(g == PASSES - 1),
+                    )
+            banks[r] = qg
+
+        def product(r):
+            qg = banks[r]
+            q_biased = work.tile([L, ROUND, QD], F32)
+            nc.vector.tensor_tensor(
+                out=q_biased[:],
+                in0=qg[:, 0:ROUND, :],
+                in1=bias_rows[:].unsqueeze(1).to_broadcast([L, ROUND, QD]),
+                op=ALU.add,
+            )
+            y = work.tile([L, ROUND, QD], F32)
+            row_sums = work.tile([L, 2, SUM_SLOT], F32)
+            for j in range(ROUND):
+                nc.vector.scalar_tensor_tensor(
+                    out=y[:, j, :],
+                    in0=q_biased[:, j, :],
+                    scalar=1.0,
+                    in1=qg[:, ROUND + j, :],
+                    op0=ALU.mult,
+                    op1=ALU.mult,
+                    accum_out=row_sums[:, 0, j : j + 1],
+                )
+            products[r] = y
+            sums[r] = row_sums
+
+        def square(r):
+            squares = work.tile([L, ROUND, QD], F32)
+            for j in range(ROUND):
+                nc.scalar.activation(
+                    out=squares[:, j, :],
+                    in_=products[r][:, j, :],
+                    func=ACT.Square,
+                    accum_out=sums[r][:, 1, j : j + 1],
+                )
+
+        def average(r):
+            moment_bank = psum_small.tile([P, 2, ROUND], F32)
+            nc.tensor.matmul(
+                out=moment_bank[:], lhsT=mean_weights[:], rhs=sums[r][:, :, 0:ROUND], start=True, stop=True
+            )
+            moments[r] = moment_bank
+
+        def spread(r):
+            minus_var = work.tile([P, ROUND], F32)
+            for j in range(ROUND):
+                nc.vector.tensor_scalar(
+                    out=minus_var[:, j : j + 1],
+                    in0=moments[r][:, 0, j : j + 1],
+                    scalar1=moments[r][:, 0, j : j + 1],
+                    scalar2=moments[r][:, 1, j : j + 1],
+                    op0=ALU.mult,
+                    op1=ALU.subtract,
+                )
+            mean = work.tile([P, ROUND], F32)
+            nc.vector.tensor_copy(out=mean[:], in_=moments[r][:, 0, :])
+            means[r] = mean
+            spreads[r] = minus_var
+
+        def inverse_deviation(r):
+            inverse = work.tile([P, ROUND], F32)
+            nc.scalar.activation(
+                out=inverse[:], in_=spreads[r][:], func=ACT.Abs_reciprocal_sqrt, scale=-1.0, bias=EPS
+            )
+            inverses[r] = inverse
+
+        def normalise(r):
+            res = res_pool.tile([L, ROUND, QD], F32)
+            for j in range(ROUND):
+                nc.vector.tensor_scalar(
+                    out=res[:, j, :],
+                    in0=products[r][:, j, :],
+                    scalar1=means[r][:, j : j + 1],
+                    scalar2=inverses[r][:, j : j + 1],
+                    op0=ALU.subtract,
+                    op1=ALU.mult,
+                )
+            nc.sync.dma_start(out=out[r * ROUND : (r + 1) * ROUND, :, :].rearrange("s l q -> l s q"), in_=res[:])
+
+        def live(r):
+            return 0 <= r < ROUNDS
+
+        decay_bank = psum_small.tile([QD, ROUND, QD], BF16, tag="kv_bank")
+        nc.tensor.transpose(decay_bank[:, 0, :], decay_rows[:], ident_bf16[:])
+        decay_turned = const.tile([QD, QD], BF16)
+        nc.vector.tensor_copy(out=decay_turned[:], in_=decay_bank[:, 0, :])
+
+        for t in range(ROUNDS + 4):
+            if live(t - 2):
+                product(t - 2)
+            if live(t - 4):
+                normalise(t - 4)
+            if live(t):
+                quantise(t, 0, turn_x(t, 0))
+                grouped_second = turn_x(t, 1)
+                turn_kv(t)
+            if live(t - 3):
+                average(t - 3)
+                spread(t - 3)
+            if live(t):
+                quantise(t, 1, grouped_second)
+            if live(t - 1):
+                multiply(t - 1)
+            if live(t - 2):
+                square(t - 2)
+            if live(t - 3):
+                inverse_deviation(t - 3)

@@ -28,6 +28,7 @@ BANK_F32 = 512
 TURNS_PER_BANK = BANK_F32 // L
 PASSES_PER_BANK = TURNS_PER_BANK // PAIRS
 BANKS_PER_SAMPLE = PASSES // PASSES_PER_BANK
+K_BANK = PASSES_PER_BANK * K_PASS
 ROUND = 2
 ROUNDS = SAMPLES // ROUND
 SCALE_ROWS = 4
@@ -43,7 +44,8 @@ def tile_parallelretention_pb_kernel(tc, x, Wq_words, Wq_scales, bq, kv, decay_m
         const = ctx.enter_context(tc.tile_pool(name="const", bufs=1))
         x_pool = ctx.enter_context(tc.tile_pool(name="x", bufs=SAMPLES * BANKS_PER_SAMPLE))
         kv_pool = ctx.enter_context(tc.tile_pool(name="kv", bufs=ROUNDS))
-        mx_pool = ctx.enter_context(tc.tile_pool(name="mx", bufs=2 * ROUND))
+        grouped_pool = ctx.enter_context(tc.tile_pool(name="grouped", bufs=4))
+        code_pool = ctx.enter_context(tc.tile_pool(name="codes", bufs=2 * ROUND * BANKS_PER_SAMPLE))
         work = ctx.enter_context(tc.tile_pool(name="work", bufs=4))
         res_pool = ctx.enter_context(tc.tile_pool(name="res", bufs=ROUNDS))
         psum_turn = ctx.enter_context(tc.psum_pool(name="psum_turn", bufs=4))
@@ -55,35 +57,39 @@ def tile_parallelretention_pb_kernel(tc, x, Wq_words, Wq_scales, bq, kv, decay_m
         make_identity(nc, ident_f32[:])
         ident_bf16 = const.tile([P, P], BF16)
         make_identity(nc, ident_bf16[:])
-        mean_weights = const.tile([P, P], F32)
-        nc.vector.memset(mean_weights[:], 1.0 / (L * QD))
+        bias_sheet = const.tile([P, QD], BF16)
+        nc.vector.memset(bias_sheet[:], 0.0)
+        ones = const.tile([P, P], BF16)
+        nc.vector.memset(ones[:], 1.0)
         w_scales = const.tile([P, PASSES, QD], U8, align_bytes=64)
         nc.vector.memset(w_scales[:].bitcast(I32), 0)
-
+        mean_weights = const.tile([P, P], F32)
+        nc.vector.memset(mean_weights[:], 1.0 / (L * QD))
         table_seed = const.tile([P, 1], F32)
         nc.vector.memset(table_seed[:], 1.0)
-        nc.scalar.activation(out=table_seed[:], in_=table_seed[:], func=ACT.Abs_reciprocal_sqrt)
 
         x_rows = {}
         kv_rows = {}
 
         def load_x(s):
             for b in range(BANKS_PER_SAMPLE):
-                x_piece = x_pool.tile([L, E // BANKS_PER_SAMPLE], BF16)
-                nc.sync.dma_start(
-                    out=x_piece[:], in_=x[s, 0, :, b * (E // BANKS_PER_SAMPLE) : (b + 1) * (E // BANKS_PER_SAMPLE)]
-                )
+                x_piece = x_pool.tile([L, K_BANK], BF16)
+                nc.sync.dma_start(out=x_piece[:], in_=x[s, 0, :, b * K_BANK : (b + 1) * K_BANK])
                 x_rows[(s, b)] = x_piece
 
-        def load_kv(r):
+        def load_kv(r, queue):
             kv_round = kv_pool.tile([L, ROUND, QD], BF16)
-            nc.sync.dma_start(
+            queue.dma_start(
                 out=kv_round[:], in_=kv[r * ROUND : (r + 1) * ROUND, 0, :, :].rearrange("s l k -> l s k")
             )
             kv_rows[r] = kv_round
 
         decay_rows = const.tile([QD, QD], BF16)
-        nc.sync.dma_start(out=decay_rows[:], in_=decay_mask[0, :, :])
+        nc.scalar.dma_start(out=decay_rows[:], in_=decay_mask[0, :, :])
+        load_kv(0, nc.scalar)
+        nc.scalar.dma_start(out=bias_sheet[0:1, :], in_=bq.unsqueeze(0))
+        nc.scalar.activation(out=table_seed[:], in_=table_seed[:], func=ACT.Abs_reciprocal_sqrt)
+
         for j in range(ROUND):
             load_x(j)
         w_words = const.tile([P, PASSES, 2 * QD], U8, align_bytes=64)
@@ -95,13 +101,10 @@ def tile_parallelretention_pb_kernel(tc, x, Wq_words, Wq_scales, bq, kv, decay_m
                     "g r w -> r g w"
                 ),
             )
-        load_kv(0)
-        bias_rows = const.tile([P, QD], BF16)
-        nc.sync.dma_start(out=bias_rows[:], in_=bq.partition_broadcast(P))
         for r in range(1, ROUNDS):
             for j in range(ROUND):
                 load_x(r * ROUND + j)
-            load_kv(r)
+            load_kv(r, nc.sync)
 
         codes = {}
         planes = {}
@@ -114,9 +117,7 @@ def tile_parallelretention_pb_kernel(tc, x, Wq_words, Wq_scales, bq, kv, decay_m
         spreads = {}
         inverses = {}
 
-        def turn_x(r, j):
-            grouped = mx_pool.tile([P, PASSES * L * PACK], BF16, align_bytes=64)
-            grouped_words = grouped[:].bitcast(F32)
+        def turn_and_quantise_x(r, j):
             for b in range(BANKS_PER_SAMPLE):
                 x_words = x_rows[(r * ROUND + j, b)][:].bitcast(F32)
                 turned = psum_turn.tile([P, TURNS_PER_BANK, L], F32)
@@ -128,20 +129,16 @@ def tile_parallelretention_pb_kernel(tc, x, Wq_words, Wq_scales, bq, kv, decay_m
                             x_words[:, first + u : first + K_PASS // 2 : PAIRS],
                             ident_f32[:],
                         )
+                grouped = grouped_pool.tile([P, PASSES_PER_BANK * L * PACK], BF16, align_bytes=64)
                 nc.scalar.copy(
-                    out=grouped_words[:, b * BANK_F32 : (b + 1) * BANK_F32].rearrange(
-                        "p (i l u) -> p i l u", i=PASSES_PER_BANK, u=PAIRS
-                    ),
+                    out=grouped[:].bitcast(F32).rearrange("p (i l u) -> p i l u", i=PASSES_PER_BANK, u=PAIRS),
                     in_=turned[:].rearrange("p (i u) l -> p i l u", u=PAIRS),
                 )
-            return grouped
-
-        def quantise(r, j, grouped):
-            x_codes = mx_pool.tile([P, PASSES * L], U32, align_bytes=64)
-            x_scales = mx_pool.tile([P, PASSES * L], U8, align_bytes=64)
-            nc.vector.quantize_mx(out=x_codes[:].bitcast(FP8X4), scales=x_scales[:], in_=grouped[:])
-            codes[(r, j)] = x_codes
-            planes[(r, j)] = x_scales
+                x_codes = code_pool.tile([P, PASSES_PER_BANK * L], U32, align_bytes=64)
+                x_scales = code_pool.tile([P, PASSES_PER_BANK * L], U8, align_bytes=64)
+                nc.vector.quantize_mx(out=x_codes[:].bitcast(FP8X4), scales=x_scales[:], in_=grouped[:])
+                codes[(r, j, b)] = x_codes
+                planes[(r, j, b)] = x_scales
 
         def turn_kv(r):
             kv_bank = psum_small.tile([QD, ROUND, L], BF16)
@@ -159,11 +156,12 @@ def tile_parallelretention_pb_kernel(tc, x, Wq_words, Wq_scales, bq, kv, decay_m
                 )
             for j in range(ROUND):
                 for g in range(PASSES):
-                    rows = slice(g * L, (g + 1) * L)
+                    b, i = divmod(g, PASSES_PER_BANK)
+                    rows = slice(i * L, (i + 1) * L)
                     nc.tensor.matmul_mx(
                         out=qg[:, j, :],
-                        lhsT=codes[(r, j)][:, rows].bitcast(FP8X4),
-                        lhsT_scale=planes[(r, j)][:, rows],
+                        lhsT=codes[(r, j, b)][:, rows].bitcast(FP8X4),
+                        lhsT_scale=planes[(r, j, b)][:, rows],
                         rhs=w_words[:, g, :].bitcast(FP4X4),
                         rhs_scale=w_scales[:, g, :],
                         start=(g == 0),
@@ -255,24 +253,26 @@ def tile_parallelretention_pb_kernel(tc, x, Wq_words, Wq_scales, bq, kv, decay_m
         nc.tensor.transpose(decay_bank[:, 0, :], decay_rows[:], ident_bf16[:])
         decay_turned = const.tile([QD, QD], BF16)
         nc.vector.tensor_copy(out=decay_turned[:], in_=decay_bank[:, 0, :])
+        bias_bank = psum_small.tile([P, QD], F32, tag="moment_bank")
+        nc.tensor.matmul(out=bias_bank[:], lhsT=ones[:], rhs=bias_sheet[:], start=True, stop=True)
+        bias_rows = const.tile([P, QD], F32)
+        nc.vector.tensor_copy(out=bias_rows[:], in_=bias_bank[:])
 
         for t in range(ROUNDS + 4):
+            if live(t - 4):
+                inverse_deviation(t - 4)
             if live(t - 2):
                 product(t - 2)
             if live(t - 4):
                 normalise(t - 4)
             if live(t):
-                quantise(t, 0, turn_x(t, 0))
-                grouped_second = turn_x(t, 1)
+                for j in range(ROUND):
+                    turn_and_quantise_x(t, j)
                 turn_kv(t)
             if live(t - 3):
                 average(t - 3)
                 spread(t - 3)
-            if live(t):
-                quantise(t, 1, grouped_second)
             if live(t - 1):
                 multiply(t - 1)
             if live(t - 2):
                 square(t - 2)
-            if live(t - 3):
-                inverse_deviation(t - 3)

@@ -42,10 +42,11 @@ def tile_parallelretention_pb_kernel(tc, x, Wq_words, Wq_scales, bq, kv, decay_m
     nc = tc.nc
     with ExitStack() as ctx:
         const = ctx.enter_context(tc.tile_pool(name="const", bufs=1))
-        x_pool = ctx.enter_context(tc.tile_pool(name="x", bufs=SAMPLES * BANKS_PER_SAMPLE))
+        x_pool = ctx.enter_context(tc.tile_pool(name="x", bufs=SAMPLES))
         kv_pool = ctx.enter_context(tc.tile_pool(name="kv", bufs=ROUNDS))
         grouped_pool = ctx.enter_context(tc.tile_pool(name="grouped", bufs=4))
-        code_pool = ctx.enter_context(tc.tile_pool(name="codes", bufs=2 * ROUND * BANKS_PER_SAMPLE))
+        code_pool = ctx.enter_context(tc.tile_pool(name="codes", bufs=SAMPLES * BANKS_PER_SAMPLE))
+        kv_turned_pool = ctx.enter_context(tc.tile_pool(name="kv_turned", bufs=ROUNDS))
         work = ctx.enter_context(tc.tile_pool(name="work", bufs=4))
         res_pool = ctx.enter_context(tc.tile_pool(name="res", bufs=ROUNDS))
         psum_turn = ctx.enter_context(tc.psum_pool(name="psum_turn", bufs=4))
@@ -72,10 +73,9 @@ def tile_parallelretention_pb_kernel(tc, x, Wq_words, Wq_scales, bq, kv, decay_m
         kv_rows = {}
 
         def load_x(s):
-            for b in range(BANKS_PER_SAMPLE):
-                x_piece = x_pool.tile([L, K_BANK], BF16)
-                nc.sync.dma_start(out=x_piece[:], in_=x[s, 0, :, b * K_BANK : (b + 1) * K_BANK])
-                x_rows[(s, b)] = x_piece
+            x_sample = x_pool.tile([L, E], BF16)
+            nc.sync.dma_start(out=x_sample[:], in_=x[s, 0, :, :])
+            x_rows[s] = x_sample
 
         def load_kv(r, queue):
             kv_round = kv_pool.tile([L, ROUND, QD], BF16)
@@ -106,6 +106,7 @@ def tile_parallelretention_pb_kernel(tc, x, Wq_words, Wq_scales, bq, kv, decay_m
                 load_x(r * ROUND + j)
             load_kv(r, nc.sync)
 
+        groups = {}
         codes = {}
         planes = {}
         kv_turned = {}
@@ -117,34 +118,38 @@ def tile_parallelretention_pb_kernel(tc, x, Wq_words, Wq_scales, bq, kv, decay_m
         spreads = {}
         inverses = {}
 
-        def turn_and_quantise_x(r, j):
-            for b in range(BANKS_PER_SAMPLE):
-                x_words = x_rows[(r * ROUND + j, b)][:].bitcast(F32)
-                turned = psum_turn.tile([P, TURNS_PER_BANK, L], F32)
-                for i in range(PASSES_PER_BANK):
-                    first = i * (K_PASS // 2)
-                    for u in range(PAIRS):
-                        nc.tensor.transpose(
-                            turned[:, i * PAIRS + u, :],
-                            x_words[:, first + u : first + K_PASS // 2 : PAIRS],
-                            ident_f32[:],
-                        )
-                grouped = grouped_pool.tile([P, PASSES_PER_BANK * L * PACK], BF16, align_bytes=64)
-                nc.scalar.copy(
-                    out=grouped[:].bitcast(F32).rearrange("p (i l u) -> p i l u", i=PASSES_PER_BANK, u=PAIRS),
-                    in_=turned[:].rearrange("p (i u) l -> p i l u", u=PAIRS),
-                )
-                x_codes = code_pool.tile([P, PASSES_PER_BANK * L], U32, align_bytes=64)
-                x_scales = code_pool.tile([P, PASSES_PER_BANK * L], U8, align_bytes=64)
-                nc.vector.quantize_mx(out=x_codes[:].bitcast(FP8X4), scales=x_scales[:], in_=grouped[:])
-                codes[(r, j, b)] = x_codes
-                planes[(r, j, b)] = x_scales
+        def turn_x(s, b):
+            x_words = x_rows[s][:].bitcast(F32)
+            turned = psum_turn.tile([P, TURNS_PER_BANK, L], F32)
+            for i in range(PASSES_PER_BANK):
+                first = (b * PASSES_PER_BANK + i) * (K_PASS // 2)
+                for u in range(PAIRS):
+                    nc.tensor.transpose(
+                        turned[:, i * PAIRS + u, :],
+                        x_words[:, first + u : first + K_PASS // 2 : PAIRS],
+                        ident_f32[:],
+                    )
+            grouped = grouped_pool.tile([P, PASSES_PER_BANK * L * PACK], BF16, align_bytes=64)
+            grouped_words = grouped[:].bitcast(F32).rearrange("p (i l u) -> p i l u", i=PASSES_PER_BANK, u=PAIRS)
+            turned_words = turned[:].rearrange("p (i u) l -> p i l u", u=PAIRS)
+            if (s * BANKS_PER_SAMPLE + b) % 4 == 3:
+                nc.vector.tensor_copy(out=grouped_words, in_=turned_words)
+            else:
+                nc.scalar.copy(out=grouped_words, in_=turned_words)
+            groups[(s, b)] = grouped
+
+        def quantise_x(s, b):
+            x_codes = code_pool.tile([P, PASSES_PER_BANK * L], U32, align_bytes=64)
+            x_scales = code_pool.tile([P, PASSES_PER_BANK * L], U8, align_bytes=64)
+            nc.vector.quantize_mx(out=x_codes[:].bitcast(FP8X4), scales=x_scales[:], in_=groups[(s, b)][:])
+            codes[(s, b)] = x_codes
+            planes[(s, b)] = x_scales
 
         def turn_kv(r):
             kv_bank = psum_small.tile([QD, ROUND, L], BF16)
             for j in range(ROUND):
                 nc.tensor.transpose(kv_bank[:, j, :], kv_rows[r][:, j, :], ident_bf16[:])
-            kv_cols = work.tile([QD, ROUND, L], BF16)
+            kv_cols = kv_turned_pool.tile([QD, ROUND, L], BF16)
             nc.vector.tensor_copy(out=kv_cols[:], in_=kv_bank[:])
             kv_turned[r] = kv_cols
 
@@ -160,8 +165,8 @@ def tile_parallelretention_pb_kernel(tc, x, Wq_words, Wq_scales, bq, kv, decay_m
                     rows = slice(i * L, (i + 1) * L)
                     nc.tensor.matmul_mx(
                         out=qg[:, j, :],
-                        lhsT=codes[(r, j, b)][:, rows].bitcast(FP8X4),
-                        lhsT_scale=planes[(r, j, b)][:, rows],
+                        lhsT=codes[(r * ROUND + j, b)][:, rows].bitcast(FP8X4),
+                        lhsT_scale=planes[(r * ROUND + j, b)][:, rows],
                         rhs=w_words[:, g, :].bitcast(FP4X4),
                         rhs_scale=w_scales[:, g, :],
                         start=(g == 0),
@@ -258,21 +263,26 @@ def tile_parallelretention_pb_kernel(tc, x, Wq_words, Wq_scales, bq, kv, decay_m
         bias_rows = const.tile([P, QD], F32)
         nc.vector.tensor_copy(out=bias_rows[:], in_=bias_bank[:])
 
-        for t in range(ROUNDS + 4):
-            if live(t - 4):
-                inverse_deviation(t - 4)
-            if live(t - 2):
-                product(t - 2)
-            if live(t - 4):
-                normalise(t - 4)
-            if live(t):
-                for j in range(ROUND):
-                    turn_and_quantise_x(t, j)
-                turn_kv(t)
-            if live(t - 3):
-                average(t - 3)
-                spread(t - 3)
-            if live(t - 1):
-                multiply(t - 1)
-            if live(t - 2):
-                square(t - 2)
+        banks_of_x = [(s, b) for s in range(SAMPLES) for b in range(BANKS_PER_SAMPLE)]
+        for n, (s, b) in enumerate(banks_of_x):
+            turn_x(s, b)
+            if n > 0:
+                quantise_x(*banks_of_x[n - 1])
+            if (n + 1) % (ROUND * BANKS_PER_SAMPLE) == 0:
+                turn_kv(n // (ROUND * BANKS_PER_SAMPLE))
+        quantise_x(*banks_of_x[-1])
+
+        for i in range(ROUNDS + 3):
+            if live(i - 3):
+                inverse_deviation(i - 3)
+            if live(i - 1):
+                product(i - 1)
+            if live(i - 3):
+                normalise(i - 3)
+            if live(i):
+                multiply(i)
+            if live(i - 2):
+                average(i - 2)
+                spread(i - 2)
+            if live(i - 1):
+                square(i - 1)

@@ -42,11 +42,10 @@ def tile_parallelretention_pb_kernel(tc, x, Wq_words, Wq_scales, bq, kv, decay_m
     nc = tc.nc
     with ExitStack() as ctx:
         const = ctx.enter_context(tc.tile_pool(name="const", bufs=1))
-        x_pool = ctx.enter_context(tc.tile_pool(name="x", bufs=SAMPLES))
+        x_pool = ctx.enter_context(tc.tile_pool(name="x", bufs=SAMPLES * BANKS_PER_SAMPLE))
         kv_pool = ctx.enter_context(tc.tile_pool(name="kv", bufs=ROUNDS))
         grouped_pool = ctx.enter_context(tc.tile_pool(name="grouped", bufs=4))
-        code_pool = ctx.enter_context(tc.tile_pool(name="codes", bufs=SAMPLES * BANKS_PER_SAMPLE))
-        kv_turned_pool = ctx.enter_context(tc.tile_pool(name="kv_turned", bufs=ROUNDS))
+        code_pool = ctx.enter_context(tc.tile_pool(name="codes", bufs=2 * ROUND * BANKS_PER_SAMPLE))
         work = ctx.enter_context(tc.tile_pool(name="work", bufs=4))
         res_pool = ctx.enter_context(tc.tile_pool(name="res", bufs=ROUNDS))
         psum_turn = ctx.enter_context(tc.psum_pool(name="psum_turn", bufs=4))
@@ -73,9 +72,10 @@ def tile_parallelretention_pb_kernel(tc, x, Wq_words, Wq_scales, bq, kv, decay_m
         kv_rows = {}
 
         def load_x(s):
-            x_sample = x_pool.tile([L, E], BF16)
-            nc.sync.dma_start(out=x_sample[:], in_=x[s, 0, :, :])
-            x_rows[s] = x_sample
+            for b in range(BANKS_PER_SAMPLE):
+                x_piece = x_pool.tile([L, K_BANK], BF16)
+                nc.sync.dma_start(out=x_piece[:], in_=x[s, 0, :, b * K_BANK : (b + 1) * K_BANK])
+                x_rows[(s, b)] = x_piece
 
         def load_kv(r, queue):
             kv_round = kv_pool.tile([L, ROUND, QD], BF16)
@@ -118,11 +118,11 @@ def tile_parallelretention_pb_kernel(tc, x, Wq_words, Wq_scales, bq, kv, decay_m
         spreads = {}
         inverses = {}
 
-        def turn_x(s, b):
-            x_words = x_rows[s][:].bitcast(F32)
+        def turn_x(r, j, b):
+            x_words = x_rows[(r * ROUND + j, b)][:].bitcast(F32)
             turned = psum_turn.tile([P, TURNS_PER_BANK, L], F32)
             for i in range(PASSES_PER_BANK):
-                first = (b * PASSES_PER_BANK + i) * (K_PASS // 2)
+                first = i * (K_PASS // 2)
                 for u in range(PAIRS):
                     nc.tensor.transpose(
                         turned[:, i * PAIRS + u, :],
@@ -130,26 +130,24 @@ def tile_parallelretention_pb_kernel(tc, x, Wq_words, Wq_scales, bq, kv, decay_m
                         ident_f32[:],
                     )
             grouped = grouped_pool.tile([P, PASSES_PER_BANK * L * PACK], BF16, align_bytes=64)
-            grouped_words = grouped[:].bitcast(F32).rearrange("p (i l u) -> p i l u", i=PASSES_PER_BANK, u=PAIRS)
-            turned_words = turned[:].rearrange("p (i u) l -> p i l u", u=PAIRS)
-            if (s * BANKS_PER_SAMPLE + b) % 4 == 3:
-                nc.vector.tensor_copy(out=grouped_words, in_=turned_words)
-            else:
-                nc.scalar.copy(out=grouped_words, in_=turned_words)
-            groups[(s, b)] = grouped
+            nc.scalar.copy(
+                out=grouped[:].bitcast(F32).rearrange("p (i l u) -> p i l u", i=PASSES_PER_BANK, u=PAIRS),
+                in_=turned[:].rearrange("p (i u) l -> p i l u", u=PAIRS),
+            )
+            groups[(r, j, b)] = grouped
 
-        def quantise_x(s, b):
+        def quantise_x(r, j, b):
             x_codes = code_pool.tile([P, PASSES_PER_BANK * L], U32, align_bytes=64)
             x_scales = code_pool.tile([P, PASSES_PER_BANK * L], U8, align_bytes=64)
-            nc.vector.quantize_mx(out=x_codes[:].bitcast(FP8X4), scales=x_scales[:], in_=groups[(s, b)][:])
-            codes[(s, b)] = x_codes
-            planes[(s, b)] = x_scales
+            nc.vector.quantize_mx(out=x_codes[:].bitcast(FP8X4), scales=x_scales[:], in_=groups[(r, j, b)][:])
+            codes[(r, j, b)] = x_codes
+            planes[(r, j, b)] = x_scales
 
         def turn_kv(r):
             kv_bank = psum_small.tile([QD, ROUND, L], BF16)
             for j in range(ROUND):
                 nc.tensor.transpose(kv_bank[:, j, :], kv_rows[r][:, j, :], ident_bf16[:])
-            kv_cols = kv_turned_pool.tile([QD, ROUND, L], BF16)
+            kv_cols = work.tile([QD, ROUND, L], BF16)
             nc.vector.tensor_copy(out=kv_cols[:], in_=kv_bank[:])
             kv_turned[r] = kv_cols
 
@@ -165,8 +163,8 @@ def tile_parallelretention_pb_kernel(tc, x, Wq_words, Wq_scales, bq, kv, decay_m
                     rows = slice(i * L, (i + 1) * L)
                     nc.tensor.matmul_mx(
                         out=qg[:, j, :],
-                        lhsT=codes[(r * ROUND + j, b)][:, rows].bitcast(FP8X4),
-                        lhsT_scale=planes[(r * ROUND + j, b)][:, rows],
+                        lhsT=codes[(r, j, b)][:, rows].bitcast(FP8X4),
+                        lhsT_scale=planes[(r, j, b)][:, rows],
                         rhs=w_words[:, g, :].bitcast(FP4X4),
                         rhs_scale=w_scales[:, g, :],
                         start=(g == 0),
@@ -263,26 +261,29 @@ def tile_parallelretention_pb_kernel(tc, x, Wq_words, Wq_scales, bq, kv, decay_m
         bias_rows = const.tile([P, QD], F32)
         nc.vector.tensor_copy(out=bias_rows[:], in_=bias_bank[:])
 
-        banks_of_x = [(s, b) for s in range(SAMPLES) for b in range(BANKS_PER_SAMPLE)]
-        for n, (s, b) in enumerate(banks_of_x):
-            turn_x(s, b)
-            if n > 0:
-                quantise_x(*banks_of_x[n - 1])
-            if (n + 1) % (ROUND * BANKS_PER_SAMPLE) == 0:
-                turn_kv(n // (ROUND * BANKS_PER_SAMPLE))
-        quantise_x(*banks_of_x[-1])
-
-        for i in range(ROUNDS + 3):
-            if live(i - 3):
-                inverse_deviation(i - 3)
-            if live(i - 1):
-                product(i - 1)
-            if live(i - 3):
-                normalise(i - 3)
-            if live(i):
-                multiply(i)
-            if live(i - 2):
-                average(i - 2)
-                spread(i - 2)
-            if live(i - 1):
-                square(i - 1)
+        last = ROUND - 1
+        for t in range(ROUNDS + 4):
+            if live(t - 2):
+                product(t - 2)
+            if live(t - 4):
+                normalise(t - 4)
+            if live(t):
+                for j in range(last):
+                    for b in range(BANKS_PER_SAMPLE):
+                        turn_x(t, j, b)
+                        quantise_x(t, j, b)
+                for b in range(BANKS_PER_SAMPLE):
+                    turn_x(t, last, b)
+                turn_kv(t)
+            if live(t - 3):
+                average(t - 3)
+                spread(t - 3)
+            if live(t):
+                for b in range(BANKS_PER_SAMPLE):
+                    quantise_x(t, last, b)
+            if live(t - 1):
+                multiply(t - 1)
+            if live(t - 2):
+                square(t - 2)
+            if live(t - 3):
+                inverse_deviation(t - 3)

@@ -38,12 +38,25 @@ SUM_SLOT = 8
 FLOPS = 2 * SAMPLES * L * E * QD + 2 * SAMPLES * L * QD * QD
 
 
+KV_ON_SCALAR = False
+NORM_ON_SCALAR = False
+SHIFT_ENGINE = "gpsimd"
+WIDE_Q = False
+BIAS_GAP = False
+SORTED_BANKS = ()
+G_AFTER_MX = True
+NORM_TOP = True
+SMALL_FIRST = False
+TAIL_SPLIT = False
+
+
 def tile_parallelretention_pb_kernel(tc, x, Wq_words, Wq_scales, bq, kv, decay_mask, out):
     nc = tc.nc
     with ExitStack() as ctx:
         const = ctx.enter_context(tc.tile_pool(name="const", bufs=1))
         x_pool = ctx.enter_context(tc.tile_pool(name="x", bufs=SAMPLES * BANKS_PER_SAMPLE))
         kv_pool = ctx.enter_context(tc.tile_pool(name="kv", bufs=ROUNDS))
+        sorted_pool = ctx.enter_context(tc.tile_pool(name="sorted", bufs=4))
         grouped_pool = ctx.enter_context(tc.tile_pool(name="grouped", bufs=4))
         code_pool = ctx.enter_context(tc.tile_pool(name="codes", bufs=2 * ROUND * BANKS_PER_SAMPLE))
         work = ctx.enter_context(tc.tile_pool(name="work", bufs=4))
@@ -74,7 +87,13 @@ def tile_parallelretention_pb_kernel(tc, x, Wq_words, Wq_scales, bq, kv, decay_m
         def load_x(s):
             for b in range(BANKS_PER_SAMPLE):
                 x_piece = x_pool.tile([L, K_BANK], BF16)
-                nc.sync.dma_start(out=x_piece[:], in_=x[s, 0, :, b * K_BANK : (b + 1) * K_BANK])
+                if SMALL_FIRST and s == 0 and b == 0:
+                    for i in range(PASSES_PER_BANK):
+                        nc.sync.dma_start(
+                            out=x_piece[:, i * K_PASS : (i + 1) * K_PASS], in_=x[s, 0, :, i * K_PASS : (i + 1) * K_PASS]
+                        )
+                else:
+                    nc.sync.dma_start(out=x_piece[:], in_=x[s, 0, :, b * K_BANK : (b + 1) * K_BANK])
                 x_rows[(s, b)] = x_piece
 
         def load_kv(r, queue):
@@ -106,17 +125,33 @@ def tile_parallelretention_pb_kernel(tc, x, Wq_words, Wq_scales, bq, kv, decay_m
                 load_x(r * ROUND + j)
             load_kv(r, nc.sync)
 
+        ordered = {}
         groups = {}
         codes = {}
         planes = {}
         kv_turned = {}
         banks = {}
+        biased = {}
         products = {}
         sums = {}
         moments = {}
         means = {}
         spreads = {}
         inverses = {}
+        shifts = {}
+        last_round = ROUNDS - 1
+
+        def on_scalar(r):
+            return NORM_ON_SCALAR and r != last_round
+
+        def sort_x(r, j, b):
+            x_words = x_rows[(r * ROUND + j, b)][:].bitcast(F32)
+            in_order = sorted_pool.tile([L, TURNS_PER_BANK, P], F32)
+            nc.vector.tensor_copy(
+                out=in_order[:].rearrange("l (i u) p -> l i u p", u=PAIRS),
+                in_=x_words.rearrange("l (i p u) -> l i u p", i=PASSES_PER_BANK, u=PAIRS),
+            )
+            ordered[(r, j, b)] = in_order
 
         def turn_x(r, j, b):
             x_words = x_rows[(r * ROUND + j, b)][:].bitcast(F32)
@@ -124,69 +159,104 @@ def tile_parallelretention_pb_kernel(tc, x, Wq_words, Wq_scales, bq, kv, decay_m
             for i in range(PASSES_PER_BANK):
                 first = i * (K_PASS // 2)
                 for u in range(PAIRS):
-                    nc.tensor.transpose(
-                        turned[:, i * PAIRS + u, :],
-                        x_words[:, first + u : first + K_PASS // 2 : PAIRS],
-                        ident_f32[:],
-                    )
-            grouped = grouped_pool.tile([P, PASSES_PER_BANK * L * PACK], BF16, align_bytes=64)
+                    if (r, j, b) in ordered:
+                        source = ordered[(r, j, b)][:, i * PAIRS + u, :]
+                    else:
+                        source = x_words[:, first + u : first + K_PASS // 2 : PAIRS]
+                    nc.tensor.transpose(turned[:, i * PAIRS + u, :], source, ident_f32[:])
+            width = PASSES_PER_BANK * L * PACK
+            if WIDE_Q:
+                if b == 0:
+                    sample_group = grouped_pool.tile([P, BANKS_PER_SAMPLE * width], BF16, align_bytes=64)
+                    groups[(r, j)] = sample_group
+                target = groups[(r, j)][:, b * width : (b + 1) * width]
+            else:
+                grouped = grouped_pool.tile([P, width], BF16, align_bytes=64)
+                groups[(r, j, b)] = grouped
+                target = grouped[:]
             nc.scalar.copy(
-                out=grouped[:].bitcast(F32).rearrange("p (i l u) -> p i l u", i=PASSES_PER_BANK, u=PAIRS),
+                out=target.bitcast(F32).rearrange("p (i l u) -> p i l u", i=PASSES_PER_BANK, u=PAIRS),
                 in_=turned[:].rearrange("p (i u) l -> p i l u", u=PAIRS),
             )
-            groups[(r, j, b)] = grouped
 
         def quantise_x(r, j, b):
-            x_codes = code_pool.tile([P, PASSES_PER_BANK * L], U32, align_bytes=64)
-            x_scales = code_pool.tile([P, PASSES_PER_BANK * L], U8, align_bytes=64)
-            nc.vector.quantize_mx(out=x_codes[:].bitcast(FP8X4), scales=x_scales[:], in_=groups[(r, j, b)][:])
-            codes[(r, j, b)] = x_codes
-            planes[(r, j, b)] = x_scales
+            if WIDE_Q:
+                if b != BANKS_PER_SAMPLE - 1:
+                    return
+                x_codes = code_pool.tile([P, PASSES * L], U32, align_bytes=64)
+                x_scales = code_pool.tile([P, PASSES * L], U8, align_bytes=64)
+                nc.vector.quantize_mx(out=x_codes[:].bitcast(FP8X4), scales=x_scales[:], in_=groups[(r, j)][:])
+                codes[(r, j)] = x_codes
+                planes[(r, j)] = x_scales
+            else:
+                x_codes = code_pool.tile([P, PASSES_PER_BANK * L], U32, align_bytes=64)
+                x_scales = code_pool.tile([P, PASSES_PER_BANK * L], U8, align_bytes=64)
+                nc.vector.quantize_mx(out=x_codes[:].bitcast(FP8X4), scales=x_scales[:], in_=groups[(r, j, b)][:])
+                codes[(r, j, b)] = x_codes
+                planes[(r, j, b)] = x_scales
 
         def turn_kv(r):
             kv_bank = psum_small.tile([QD, ROUND, L], BF16)
             for j in range(ROUND):
                 nc.tensor.transpose(kv_bank[:, j, :], kv_rows[r][:, j, :], ident_bf16[:])
             kv_cols = work.tile([QD, ROUND, L], BF16)
-            nc.vector.tensor_copy(out=kv_cols[:], in_=kv_bank[:])
+            if KV_ON_SCALAR:
+                nc.scalar.copy(out=kv_cols[:], in_=kv_bank[:])
+            else:
+                nc.vector.tensor_copy(out=kv_cols[:], in_=kv_bank[:])
             kv_turned[r] = kv_cols
 
         def multiply(r):
             qg = psum_qg.tile([L, 2 * ROUND, QD], F32)
-            for j in range(ROUND):
-                nc.tensor.matmul(
-                    out=qg[:, ROUND + j, :], lhsT=kv_turned[r][:, j, :], rhs=decay_turned[:], start=True, stop=True
-                )
+            g_last = G_AFTER_MX and live(r + 2)
+
+            def plain():
+                for j in range(ROUND):
+                    nc.tensor.matmul(
+                        out=qg[:, ROUND + j, :], lhsT=kv_turned[r][:, j, :], rhs=decay_turned[:], start=True, stop=True
+                    )
+
+            if not g_last:
+                plain()
             for j in range(ROUND):
                 for g in range(PASSES):
-                    b, i = divmod(g, PASSES_PER_BANK)
+                    if WIDE_Q:
+                        code_tile, plane_tile, i = codes[(r, j)], planes[(r, j)], g
+                    else:
+                        b, i = divmod(g, PASSES_PER_BANK)
+                        code_tile, plane_tile = codes[(r, j, b)], planes[(r, j, b)]
                     rows = slice(i * L, (i + 1) * L)
                     nc.tensor.matmul_mx(
                         out=qg[:, j, :],
-                        lhsT=codes[(r, j, b)][:, rows].bitcast(FP8X4),
-                        lhsT_scale=planes[(r, j, b)][:, rows],
+                        lhsT=code_tile[:, rows].bitcast(FP8X4),
+                        lhsT_scale=plane_tile[:, rows],
                         rhs=w_words[:, g, :].bitcast(FP4X4),
                         rhs_scale=w_scales[:, g, :],
                         start=(g == 0),
                         stop=(g == PASSES - 1),
                     )
+            if g_last:
+                plain()
             banks[r] = qg
 
-        def product(r):
-            qg = banks[r]
+        def add_bias(r):
             q_biased = work.tile([L, ROUND, QD], F32)
             nc.vector.tensor_tensor(
                 out=q_biased[:],
-                in0=qg[:, 0:ROUND, :],
+                in0=banks[r][:, 0:ROUND, :],
                 in1=bias_rows[:].unsqueeze(1).to_broadcast([L, ROUND, QD]),
                 op=ALU.add,
             )
+            biased[r] = q_biased
+
+        def product(r):
+            qg = banks[r]
             y = work.tile([L, ROUND, QD], F32)
             row_sums = work.tile([L, 2, SUM_SLOT], F32)
             for j in range(ROUND):
                 nc.vector.scalar_tensor_tensor(
                     out=y[:, j, :],
-                    in0=q_biased[:, j, :],
+                    in0=biased[r][:, j, :],
                     scalar=1.0,
                     in1=qg[:, ROUND + j, :],
                     op0=ALU.mult,
@@ -225,7 +295,10 @@ def tile_parallelretention_pb_kernel(tc, x, Wq_words, Wq_scales, bq, kv, decay_m
                     op1=ALU.subtract,
                 )
             mean = work.tile([P, ROUND], F32)
-            nc.vector.tensor_copy(out=mean[:], in_=moments[r][:, 0, :])
+            if on_scalar(r):
+                nc.vector.tensor_scalar(out=mean[:], in0=moments[r][:, 0, :], scalar1=-1.0, scalar2=None, op0=ALU.mult)
+            else:
+                nc.vector.tensor_copy(out=mean[:], in_=moments[r][:, 0, :])
             means[r] = mean
             spreads[r] = minus_var
 
@@ -235,18 +308,34 @@ def tile_parallelretention_pb_kernel(tc, x, Wq_words, Wq_scales, bq, kv, decay_m
                 out=inverse[:], in_=spreads[r][:], func=ACT.Abs_reciprocal_sqrt, scale=-1.0, bias=EPS
             )
             inverses[r] = inverse
+            if on_scalar(r):
+                shift = work.tile([P, ROUND], F32)
+                if SHIFT_ENGINE == "gpsimd":
+                    nc.gpsimd.tensor_tensor(out=shift[:], in0=means[r][:], in1=inverse[:], op=ALU.mult)
+                else:
+                    nc.vector.tensor_tensor(out=shift[:], in0=means[r][:], in1=inverse[:], op=ALU.mult)
+                shifts[r] = shift
 
         def normalise(r):
             res = res_pool.tile([L, ROUND, QD], F32)
             for j in range(ROUND):
-                nc.vector.tensor_scalar(
-                    out=res[:, j, :],
-                    in0=products[r][:, j, :],
-                    scalar1=means[r][:, j : j + 1],
-                    scalar2=inverses[r][:, j : j + 1],
-                    op0=ALU.subtract,
-                    op1=ALU.mult,
-                )
+                if on_scalar(r):
+                    nc.scalar.activation(
+                        out=res[:, j, :],
+                        in_=products[r][:, j, :],
+                        func=ACT.Identity,
+                        scale=inverses[r][:, j : j + 1],
+                        bias=shifts[r][:, j : j + 1],
+                    )
+                else:
+                    nc.vector.tensor_scalar(
+                        out=res[:, j, :],
+                        in0=products[r][:, j, :],
+                        scalar1=means[r][:, j : j + 1],
+                        scalar2=inverses[r][:, j : j + 1],
+                        op0=ALU.subtract,
+                        op1=ALU.mult,
+                    )
             nc.sync.dma_start(out=out[r * ROUND : (r + 1) * ROUND, :, :].rearrange("s l q -> l s q"), in_=res[:])
 
         def live(r):
@@ -262,11 +351,24 @@ def tile_parallelretention_pb_kernel(tc, x, Wq_words, Wq_scales, bq, kv, decay_m
         nc.vector.tensor_copy(out=bias_rows[:], in_=bias_bank[:])
 
         last = ROUND - 1
+
+        def sorts(r):
+            if live(r):
+                for j in range(ROUND):
+                    for b in SORTED_BANKS:
+                        sort_x(r, j, b)
+
         for t in range(ROUNDS + 4):
+            if t > 0:
+                sorts(t + 1)
             if live(t - 2):
-                product(t - 2)
+                add_bias(t - 2)
+                if not BIAS_GAP:
+                    product(t - 2)
             if live(t - 4):
                 normalise(t - 4)
+            if live(t - 2) and BIAS_GAP:
+                product(t - 2)
             if live(t):
                 for j in range(last):
                     for b in range(BANKS_PER_SAMPLE):
@@ -278,6 +380,8 @@ def tile_parallelretention_pb_kernel(tc, x, Wq_words, Wq_scales, bq, kv, decay_m
             if live(t - 3):
                 average(t - 3)
                 spread(t - 3)
+            if t == 0:
+                sorts(t + 1)
             if live(t):
                 for b in range(BANKS_PER_SAMPLE):
                     quantise_x(t, last, b)

@@ -38,6 +38,7 @@ SUM_SLOT = 8
 FLOPS = 2 * SAMPLES * L * E * QD + 2 * SAMPLES * L * QD * QD
 
 
+SPLIT_SAMPLES = 4
 KV_ON_SCALAR = False
 NORM_ON_SCALAR = False
 SHIFT_ENGINE = "gpsimd"
@@ -54,7 +55,7 @@ def tile_parallelretention_pb_kernel(tc, x, Wq_words, Wq_scales, bq, kv, decay_m
     nc = tc.nc
     with ExitStack() as ctx:
         const = ctx.enter_context(tc.tile_pool(name="const", bufs=1))
-        x_pool = ctx.enter_context(tc.tile_pool(name="x", bufs=SAMPLES * BANKS_PER_SAMPLE))
+        x_pool = ctx.enter_context(tc.tile_pool(name="x", bufs=SAMPLES))
         kv_pool = ctx.enter_context(tc.tile_pool(name="kv", bufs=ROUNDS))
         sorted_pool = ctx.enter_context(tc.tile_pool(name="sorted", bufs=4))
         grouped_pool = ctx.enter_context(tc.tile_pool(name="grouped", bufs=4))
@@ -85,16 +86,16 @@ def tile_parallelretention_pb_kernel(tc, x, Wq_words, Wq_scales, bq, kv, decay_m
         kv_rows = {}
 
         def load_x(s):
+            x_sample = x_pool.tile([L, E], BF16)
+            if s < SPLIT_SAMPLES:
+                for b in range(BANKS_PER_SAMPLE):
+                    nc.sync.dma_start(
+                        out=x_sample[:, b * K_BANK : (b + 1) * K_BANK], in_=x[s, 0, :, b * K_BANK : (b + 1) * K_BANK]
+                    )
+            else:
+                nc.sync.dma_start(out=x_sample[:], in_=x[s, 0, :, :])
             for b in range(BANKS_PER_SAMPLE):
-                x_piece = x_pool.tile([L, K_BANK], BF16)
-                if SMALL_FIRST and s == 0 and b == 0:
-                    for i in range(PASSES_PER_BANK):
-                        nc.sync.dma_start(
-                            out=x_piece[:, i * K_PASS : (i + 1) * K_PASS], in_=x[s, 0, :, i * K_PASS : (i + 1) * K_PASS]
-                        )
-                else:
-                    nc.sync.dma_start(out=x_piece[:], in_=x[s, 0, :, b * K_BANK : (b + 1) * K_BANK])
-                x_rows[(s, b)] = x_piece
+                x_rows[(s, b)] = x_sample[:, b * K_BANK : (b + 1) * K_BANK]
 
         def load_kv(r, queue):
             kv_round = kv_pool.tile([L, ROUND, QD], BF16)
@@ -145,7 +146,7 @@ def tile_parallelretention_pb_kernel(tc, x, Wq_words, Wq_scales, bq, kv, decay_m
             return NORM_ON_SCALAR and r != last_round
 
         def sort_x(r, j, b):
-            x_words = x_rows[(r * ROUND + j, b)][:].bitcast(F32)
+            x_words = x_rows[(r * ROUND + j, b)].bitcast(F32)
             in_order = sorted_pool.tile([L, TURNS_PER_BANK, P], F32)
             nc.vector.tensor_copy(
                 out=in_order[:].rearrange("l (i u) p -> l i u p", u=PAIRS),
@@ -154,7 +155,7 @@ def tile_parallelretention_pb_kernel(tc, x, Wq_words, Wq_scales, bq, kv, decay_m
             ordered[(r, j, b)] = in_order
 
         def turn_x(r, j, b):
-            x_words = x_rows[(r * ROUND + j, b)][:].bitcast(F32)
+            x_words = x_rows[(r * ROUND + j, b)].bitcast(F32)
             turned = psum_turn.tile([P, TURNS_PER_BANK, L], F32)
             for i in range(PASSES_PER_BANK):
                 first = i * (K_PASS // 2)

@@ -39,16 +39,9 @@ FLOPS = 2 * SAMPLES * L * E * QD + 2 * SAMPLES * L * QD * QD
 
 
 SPLIT_SAMPLES = 4
-KV_ON_SCALAR = False
-NORM_ON_SCALAR = False
-SHIFT_ENGINE = "gpsimd"
-WIDE_Q = False
-BIAS_GAP = False
-SORTED_BANKS = ()
-G_AFTER_MX = True
-NORM_TOP = True
-SMALL_FIRST = False
 TAIL_SPLIT = False
+HEAD = 0
+W_AFTER = 1
 
 
 def tile_parallelretention_pb_kernel(tc, x, Wq_words, Wq_scales, bq, kv, decay_mask, out):
@@ -57,10 +50,10 @@ def tile_parallelretention_pb_kernel(tc, x, Wq_words, Wq_scales, bq, kv, decay_m
         const = ctx.enter_context(tc.tile_pool(name="const", bufs=1))
         x_pool = ctx.enter_context(tc.tile_pool(name="x", bufs=SAMPLES))
         kv_pool = ctx.enter_context(tc.tile_pool(name="kv", bufs=ROUNDS))
-        sorted_pool = ctx.enter_context(tc.tile_pool(name="sorted", bufs=4))
         grouped_pool = ctx.enter_context(tc.tile_pool(name="grouped", bufs=4))
         code_pool = ctx.enter_context(tc.tile_pool(name="codes", bufs=2 * ROUND * BANKS_PER_SAMPLE))
         work = ctx.enter_context(tc.tile_pool(name="work", bufs=4))
+        y_pool = ctx.enter_context(tc.tile_pool(name="y", bufs=6))
         res_pool = ctx.enter_context(tc.tile_pool(name="res", bufs=ROUNDS))
         psum_turn = ctx.enter_context(tc.psum_pool(name="psum_turn", bufs=4))
         psum_qg = ctx.enter_context(tc.psum_pool(name="psum_qg", bufs=2))
@@ -105,33 +98,42 @@ def tile_parallelretention_pb_kernel(tc, x, Wq_words, Wq_scales, bq, kv, decay_m
             kv_rows[r] = kv_round
 
         decay_rows = const.tile([QD, QD], BF16)
-        nc.scalar.dma_start(out=decay_rows[:], in_=decay_mask[0, :, :])
-        load_kv(0, nc.scalar)
-        nc.scalar.dma_start(out=bias_sheet[0:1, :], in_=bq.unsqueeze(0))
-        nc.scalar.activation(out=table_seed[:], in_=table_seed[:], func=ACT.Abs_reciprocal_sqrt)
-
-        for j in range(ROUND):
-            load_x(j)
         w_words = const.tile([P, PASSES, 2 * QD], U8, align_bytes=64)
-        nc.sync.dma_start(out=w_words[:].bitcast(I32), in_=Wq_words.bitcast(I32).rearrange("g p w -> p g w"))
-        for quad in range(QUADRANTS):
-            nc.sync.dma_start(
-                out=w_scales[32 * quad : 32 * quad + SCALE_ROWS, :, :].bitcast(I32),
-                in_=Wq_scales.bitcast(I32)[:, SCALE_ROWS * quad : SCALE_ROWS * (quad + 1), :].rearrange(
-                    "g r w -> r g w"
-                ),
-            )
-        for r in range(1, ROUNDS):
+
+        def load_small(queue):
+            queue.dma_start(out=decay_rows[:], in_=decay_mask[0, :, :])
+            load_kv(0, queue)
+            queue.dma_start(out=bias_sheet[0:1, :], in_=bq.unsqueeze(0))
+
+        def load_w():
+            nc.sync.dma_start(out=w_words[:].bitcast(I32), in_=Wq_words.bitcast(I32).rearrange("g p w -> p g w"))
+            for quad in range(QUADRANTS):
+                nc.sync.dma_start(
+                    out=w_scales[32 * quad : 32 * quad + SCALE_ROWS, :, :].bitcast(I32),
+                    in_=Wq_scales.bitcast(I32)[:, SCALE_ROWS * quad : SCALE_ROWS * (quad + 1), :].rearrange(
+                        "g r w -> r g w"
+                    ),
+                )
+
+        if HEAD == 0:
+            load_small(nc.scalar)
+        nc.scalar.activation(out=table_seed[:], in_=table_seed[:], func=ACT.Abs_reciprocal_sqrt)
+        for r in range(ROUNDS):
             for j in range(ROUND):
                 load_x(r * ROUND + j)
-            load_kv(r, nc.sync)
+            if r == 0 and HEAD == 1:
+                load_small(nc.sync)
+            if r > 0:
+                load_kv(r, nc.sync)
+            if r + 1 == W_AFTER:
+                load_w()
 
-        ordered = {}
         groups = {}
         codes = {}
         planes = {}
         kv_turned = {}
-        banks = {}
+        q_banks = {}
+        g_banks = {}
         biased = {}
         products = {}
         sums = {}
@@ -139,20 +141,29 @@ def tile_parallelretention_pb_kernel(tc, x, Wq_words, Wq_scales, bq, kv, decay_m
         means = {}
         spreads = {}
         inverses = {}
-        shifts = {}
+        results = {}
         last_round = ROUNDS - 1
+        both = tuple(range(ROUND))
 
-        def on_scalar(r):
-            return NORM_ON_SCALAR and r != last_round
+        PAIRED = ROUNDS - 2
 
-        def sort_x(r, j, b):
-            x_words = x_rows[(r * ROUND + j, b)].bitcast(F32)
-            in_order = sorted_pool.tile([L, TURNS_PER_BANK, P], F32)
-            nc.vector.tensor_copy(
-                out=in_order[:].rearrange("l (i u) p -> l i u p", u=PAIRS),
-                in_=x_words.rearrange("l (i p u) -> l i u p", i=PASSES_PER_BANK, u=PAIRS),
-            )
-            ordered[(r, j, b)] = in_order
+        def group(r):
+            return r // 2 if r < PAIRED else r - PAIRED // 2
+
+        def closes_group(r):
+            return r >= PAIRED or r % 2 == 1
+
+        def width(r):
+            return 2 * ROUND if r < PAIRED else ROUND
+
+        def col(r, j):
+            return (r % 2) * ROUND + j if r < PAIRED else j
+
+        def split(r):
+            return TAIL_SPLIT and r == last_round
+
+        def live(r):
+            return 0 <= r < ROUNDS
 
         def turn_x(r, j, b):
             x_words = x_rows[(r * ROUND + j, b)].bitcast(F32)
@@ -160,77 +171,63 @@ def tile_parallelretention_pb_kernel(tc, x, Wq_words, Wq_scales, bq, kv, decay_m
             for i in range(PASSES_PER_BANK):
                 first = i * (K_PASS // 2)
                 for u in range(PAIRS):
-                    if (r, j, b) in ordered:
-                        source = ordered[(r, j, b)][:, i * PAIRS + u, :]
-                    else:
-                        source = x_words[:, first + u : first + K_PASS // 2 : PAIRS]
-                    nc.tensor.transpose(turned[:, i * PAIRS + u, :], source, ident_f32[:])
-            width = PASSES_PER_BANK * L * PACK
-            if WIDE_Q:
-                if b == 0:
-                    sample_group = grouped_pool.tile([P, BANKS_PER_SAMPLE * width], BF16, align_bytes=64)
-                    groups[(r, j)] = sample_group
-                target = groups[(r, j)][:, b * width : (b + 1) * width]
-            else:
-                grouped = grouped_pool.tile([P, width], BF16, align_bytes=64)
-                groups[(r, j, b)] = grouped
-                target = grouped[:]
+                    nc.tensor.transpose(
+                        turned[:, i * PAIRS + u, :],
+                        x_words[:, first + u : first + K_PASS // 2 : PAIRS],
+                        ident_f32[:],
+                    )
+            grouped = grouped_pool.tile([P, PASSES_PER_BANK * L * PACK], BF16, align_bytes=64)
             nc.scalar.copy(
-                out=target.bitcast(F32).rearrange("p (i l u) -> p i l u", i=PASSES_PER_BANK, u=PAIRS),
+                out=grouped[:].bitcast(F32).rearrange("p (i l u) -> p i l u", i=PASSES_PER_BANK, u=PAIRS),
                 in_=turned[:].rearrange("p (i u) l -> p i l u", u=PAIRS),
             )
+            groups[(r, j, b)] = grouped
 
         def quantise_x(r, j, b):
-            if WIDE_Q:
-                if b != BANKS_PER_SAMPLE - 1:
-                    return
-                x_codes = code_pool.tile([P, PASSES * L], U32, align_bytes=64)
-                x_scales = code_pool.tile([P, PASSES * L], U8, align_bytes=64)
-                nc.vector.quantize_mx(out=x_codes[:].bitcast(FP8X4), scales=x_scales[:], in_=groups[(r, j)][:])
-                codes[(r, j)] = x_codes
-                planes[(r, j)] = x_scales
-            else:
-                x_codes = code_pool.tile([P, PASSES_PER_BANK * L], U32, align_bytes=64)
-                x_scales = code_pool.tile([P, PASSES_PER_BANK * L], U8, align_bytes=64)
-                nc.vector.quantize_mx(out=x_codes[:].bitcast(FP8X4), scales=x_scales[:], in_=groups[(r, j, b)][:])
-                codes[(r, j, b)] = x_codes
-                planes[(r, j, b)] = x_scales
+            x_codes = code_pool.tile([P, PASSES_PER_BANK * L], U32, align_bytes=64)
+            x_scales = code_pool.tile([P, PASSES_PER_BANK * L], U8, align_bytes=64)
+            nc.vector.quantize_mx(out=x_codes[:].bitcast(FP8X4), scales=x_scales[:], in_=groups[(r, j, b)][:])
+            codes[(r, j, b)] = x_codes
+            planes[(r, j, b)] = x_scales
 
         def turn_kv(r):
             kv_bank = psum_small.tile([QD, ROUND, L], BF16)
             for j in range(ROUND):
                 nc.tensor.transpose(kv_bank[:, j, :], kv_rows[r][:, j, :], ident_bf16[:])
             kv_cols = work.tile([QD, ROUND, L], BF16)
-            if KV_ON_SCALAR:
-                nc.scalar.copy(out=kv_cols[:], in_=kv_bank[:])
-            else:
-                nc.vector.tensor_copy(out=kv_cols[:], in_=kv_bank[:])
+            nc.vector.tensor_copy(out=kv_cols[:], in_=kv_bank[:])
             kv_turned[r] = kv_cols
 
         def multiply(r):
-            qg = psum_qg.tile([L, 2 * ROUND, QD], F32)
-            g_last = G_AFTER_MX and live(r + 2)
+            if split(r):
+                for j in both:
+                    own = psum_turn.tile([L, 2 * ROUND, QD], F32, tag="turned")
+                    q_banks[(r, j)] = own[:, 0, :]
+                    g_banks[(r, j)] = own[:, 1, :]
+            else:
+                qg = psum_qg.tile([L, 2 * ROUND, QD], F32)
+                for j in both:
+                    q_banks[(r, j)] = qg[:, j, :]
+                    g_banks[(r, j)] = qg[:, ROUND + j, :]
+                q_banks[r] = qg[:, 0:ROUND, :]
+            g_last = live(r + 2)
 
             def plain():
-                for j in range(ROUND):
+                for j in both:
                     nc.tensor.matmul(
-                        out=qg[:, ROUND + j, :], lhsT=kv_turned[r][:, j, :], rhs=decay_turned[:], start=True, stop=True
+                        out=g_banks[(r, j)], lhsT=kv_turned[r][:, j, :], rhs=decay_turned[:], start=True, stop=True
                     )
 
             if not g_last:
                 plain()
-            for j in range(ROUND):
+            for j in both:
                 for g in range(PASSES):
-                    if WIDE_Q:
-                        code_tile, plane_tile, i = codes[(r, j)], planes[(r, j)], g
-                    else:
-                        b, i = divmod(g, PASSES_PER_BANK)
-                        code_tile, plane_tile = codes[(r, j, b)], planes[(r, j, b)]
+                    b, i = divmod(g, PASSES_PER_BANK)
                     rows = slice(i * L, (i + 1) * L)
                     nc.tensor.matmul_mx(
-                        out=qg[:, j, :],
-                        lhsT=code_tile[:, rows].bitcast(FP8X4),
-                        lhsT_scale=plane_tile[:, rows],
+                        out=q_banks[(r, j)],
+                        lhsT=codes[(r, j, b)][:, rows].bitcast(FP8X4),
+                        lhsT_scale=planes[(r, j, b)][:, rows],
                         rhs=w_words[:, g, :].bitcast(FP4X4),
                         rhs_scale=w_scales[:, g, :],
                         start=(g == 0),
@@ -238,138 +235,120 @@ def tile_parallelretention_pb_kernel(tc, x, Wq_words, Wq_scales, bq, kv, decay_m
                     )
             if g_last:
                 plain()
-            banks[r] = qg
 
-        def add_bias(r):
-            q_biased = work.tile([L, ROUND, QD], F32)
-            nc.vector.tensor_tensor(
-                out=q_biased[:],
-                in0=banks[r][:, 0:ROUND, :],
-                in1=bias_rows[:].unsqueeze(1).to_broadcast([L, ROUND, QD]),
-                op=ALU.add,
-            )
-            biased[r] = q_biased
+        def add_bias(r, js):
+            if r not in biased:
+                q_biased = work.tile([L, ROUND, QD], F32)
+                biased[r] = q_biased
+            if js == both:
+                nc.vector.tensor_tensor(
+                    out=biased[r][:],
+                    in0=q_banks[r],
+                    in1=bias_rows[:].unsqueeze(1).to_broadcast([L, ROUND, QD]),
+                    op=ALU.add,
+                )
+            else:
+                for j in js:
+                    nc.vector.tensor_tensor(out=biased[r][:, j, :], in0=q_banks[(r, j)], in1=bias_rows[:], op=ALU.add)
 
-        def product(r):
-            qg = banks[r]
-            y = work.tile([L, ROUND, QD], F32)
-            row_sums = work.tile([L, 2, SUM_SLOT], F32)
-            for j in range(ROUND):
+        def product(r, js):
+            if r not in products:
+                y = y_pool.tile([L, ROUND, QD], F32)
+                products[r] = y
+            if group(r) not in sums:
+                row_sums = work.tile([L, 2, SUM_SLOT], F32)
+                sums[group(r)] = row_sums
+            for j in js:
                 nc.vector.scalar_tensor_tensor(
-                    out=y[:, j, :],
+                    out=products[r][:, j, :],
                     in0=biased[r][:, j, :],
                     scalar=1.0,
-                    in1=qg[:, ROUND + j, :],
+                    in1=g_banks[(r, j)],
                     op0=ALU.mult,
                     op1=ALU.mult,
-                    accum_out=row_sums[:, 0, j : j + 1],
+                    accum_out=sums[group(r)][:, 0, col(r, j) : col(r, j) + 1],
                 )
-            products[r] = y
-            sums[r] = row_sums
 
-        def square(r):
-            squares = work.tile([L, ROUND, QD], F32)
-            for j in range(ROUND):
+        def square(r, js):
+            for j in js:
+                squares = work.tile([L, QD], F32)
                 nc.scalar.activation(
-                    out=squares[:, j, :],
+                    out=squares[:],
                     in_=products[r][:, j, :],
                     func=ACT.Square,
-                    accum_out=sums[r][:, 1, j : j + 1],
+                    accum_out=sums[group(r)][:, 1, col(r, j) : col(r, j) + 1],
                 )
 
         def average(r):
-            moment_bank = psum_small.tile([P, 2, ROUND], F32)
+            moment_bank = psum_small.tile([P, 2, width(r)], F32)
             nc.tensor.matmul(
-                out=moment_bank[:], lhsT=mean_weights[:], rhs=sums[r][:, :, 0:ROUND], start=True, stop=True
+                out=moment_bank[:], lhsT=mean_weights[:], rhs=sums[group(r)][:, :, 0 : width(r)], start=True, stop=True
             )
-            moments[r] = moment_bank
+            moments[group(r)] = moment_bank
 
         def spread(r):
-            minus_var = work.tile([P, ROUND], F32)
-            for j in range(ROUND):
+            minus_var = work.tile([P, width(r)], F32)
+            bank = moments[group(r)]
+            for c in range(width(r)):
                 nc.vector.tensor_scalar(
-                    out=minus_var[:, j : j + 1],
-                    in0=moments[r][:, 0, j : j + 1],
-                    scalar1=moments[r][:, 0, j : j + 1],
-                    scalar2=moments[r][:, 1, j : j + 1],
+                    out=minus_var[:, c : c + 1],
+                    in0=bank[:, 0, c : c + 1],
+                    scalar1=bank[:, 0, c : c + 1],
+                    scalar2=bank[:, 1, c : c + 1],
                     op0=ALU.mult,
                     op1=ALU.subtract,
                 )
-            mean = work.tile([P, ROUND], F32)
-            if on_scalar(r):
-                nc.vector.tensor_scalar(out=mean[:], in0=moments[r][:, 0, :], scalar1=-1.0, scalar2=None, op0=ALU.mult)
-            else:
-                nc.vector.tensor_copy(out=mean[:], in_=moments[r][:, 0, :])
-            means[r] = mean
-            spreads[r] = minus_var
+            mean = work.tile([P, width(r)], F32)
+            nc.vector.tensor_copy(out=mean[:], in_=bank[:, 0, :])
+            means[group(r)] = mean
+            spreads[group(r)] = minus_var
 
         def inverse_deviation(r):
-            inverse = work.tile([P, ROUND], F32)
+            inverse = work.tile([P, width(r)], F32)
             nc.scalar.activation(
-                out=inverse[:], in_=spreads[r][:], func=ACT.Abs_reciprocal_sqrt, scale=-1.0, bias=EPS
+                out=inverse[:], in_=spreads[group(r)][:], func=ACT.Abs_reciprocal_sqrt, scale=-1.0, bias=EPS
             )
-            inverses[r] = inverse
-            if on_scalar(r):
-                shift = work.tile([P, ROUND], F32)
-                if SHIFT_ENGINE == "gpsimd":
-                    nc.gpsimd.tensor_tensor(out=shift[:], in0=means[r][:], in1=inverse[:], op=ALU.mult)
-                else:
-                    nc.vector.tensor_tensor(out=shift[:], in0=means[r][:], in1=inverse[:], op=ALU.mult)
-                shifts[r] = shift
+            inverses[group(r)] = inverse
 
         def normalise(r):
             res = res_pool.tile([L, ROUND, QD], F32)
-            for j in range(ROUND):
-                if on_scalar(r):
-                    nc.scalar.activation(
-                        out=res[:, j, :],
-                        in_=products[r][:, j, :],
-                        func=ACT.Identity,
-                        scale=inverses[r][:, j : j + 1],
-                        bias=shifts[r][:, j : j + 1],
-                    )
-                else:
-                    nc.vector.tensor_scalar(
-                        out=res[:, j, :],
-                        in0=products[r][:, j, :],
-                        scalar1=means[r][:, j : j + 1],
-                        scalar2=inverses[r][:, j : j + 1],
-                        op0=ALU.subtract,
-                        op1=ALU.mult,
-                    )
+            for j in both:
+                c = col(r, j)
+                nc.vector.tensor_scalar(
+                    out=res[:, j, :],
+                    in0=products[r][:, j, :],
+                    scalar1=means[group(r)][:, c : c + 1],
+                    scalar2=inverses[group(r)][:, c : c + 1],
+                    op0=ALU.subtract,
+                    op1=ALU.mult,
+                )
             nc.sync.dma_start(out=out[r * ROUND : (r + 1) * ROUND, :, :].rearrange("s l q -> l s q"), in_=res[:])
 
-        def live(r):
-            return 0 <= r < ROUNDS
+        def make_constants():
+            decay_bank = psum_small.tile([QD, ROUND, QD], BF16, tag="kv_bank")
+            nc.tensor.transpose(decay_bank[:, 0, :], decay_rows[:], ident_bf16[:])
+            nc.vector.tensor_copy(out=decay_turned[:], in_=decay_bank[:, 0, :])
+            bias_bank = psum_small.tile([P, QD], F32, tag="moment_bank")
+            nc.tensor.matmul(out=bias_bank[:], lhsT=ones[:], rhs=bias_sheet[:], start=True, stop=True)
+            nc.vector.tensor_copy(out=bias_rows[:], in_=bias_bank[:])
 
-        decay_bank = psum_small.tile([QD, ROUND, QD], BF16, tag="kv_bank")
-        nc.tensor.transpose(decay_bank[:, 0, :], decay_rows[:], ident_bf16[:])
         decay_turned = const.tile([QD, QD], BF16)
-        nc.vector.tensor_copy(out=decay_turned[:], in_=decay_bank[:, 0, :])
-        bias_bank = psum_small.tile([P, QD], F32, tag="moment_bank")
-        nc.tensor.matmul(out=bias_bank[:], lhsT=ones[:], rhs=bias_sheet[:], start=True, stop=True)
         bias_rows = const.tile([P, QD], F32)
-        nc.vector.tensor_copy(out=bias_rows[:], in_=bias_bank[:])
+        if HEAD == 0:
+            make_constants()
 
         last = ROUND - 1
 
-        def sorts(r):
-            if live(r):
-                for j in range(ROUND):
-                    for b in SORTED_BANKS:
-                        sort_x(r, j, b)
+        def stats_due(t):
+            return live(t - 3) and closes_group(t - 3)
 
         for t in range(ROUNDS + 4):
-            if t > 0:
-                sorts(t + 1)
             if live(t - 2):
-                add_bias(t - 2)
-                if not BIAS_GAP:
-                    product(t - 2)
-            if live(t - 4):
-                normalise(t - 4)
-            if live(t - 2) and BIAS_GAP:
-                product(t - 2)
+                add_bias(t - 2, both)
+                product(t - 2, both)
+            for r in (t - 5, t - 4):
+                if live(r) and (r < PAIRED) == (r == t - 5):
+                    normalise(r)
             if live(t):
                 for j in range(last):
                     for b in range(BANKS_PER_SAMPLE):
@@ -378,17 +357,17 @@ def tile_parallelretention_pb_kernel(tc, x, Wq_words, Wq_scales, bq, kv, decay_m
                 for b in range(BANKS_PER_SAMPLE):
                     turn_x(t, last, b)
                 turn_kv(t)
-            if live(t - 3):
+            if live(t - 1) and not live(t):
+                multiply(t - 1)
+            if stats_due(t):
                 average(t - 3)
                 spread(t - 3)
-            if t == 0:
-                sorts(t + 1)
             if live(t):
                 for b in range(BANKS_PER_SAMPLE):
                     quantise_x(t, last, b)
-            if live(t - 1):
+            if live(t - 1) and live(t):
                 multiply(t - 1)
             if live(t - 2):
-                square(t - 2)
-            if live(t - 3):
+                square(t - 2, both)
+            if stats_due(t):
                 inverse_deviation(t - 3)

from contextlib import ExitStack

import concourse.mybir as mybir
from concourse.masks import make_identity

F32 = mybir.dt.float32
BF16 = mybir.dt.bfloat16
I32 = mybir.dt.int32
U32 = mybir.dt.uint32
U8 = mybir.dt.uint8
FP8X4 = mybir.dt.float8_e4m3fn_x4
FP4X4 = mybir.dt.float4_e2m1fn_x4
ALU = mybir.AluOpType
ACT = mybir.ActivationFunctionType

SAMPLES = 16
L = 128
E = 2048
QD = 128
EPS = 1e-5

P = 128
PACK = 4
K_PASS = P * PACK
PASSES = E // K_PASS
PAIRS = 2
BANK_F32 = 512
TURNS_PER_BANK = BANK_F32 // L
PASSES_PER_BANK = TURNS_PER_BANK // PAIRS
BANKS_PER_SAMPLE = PASSES // PASSES_PER_BANK
K_BANK = PASSES_PER_BANK * K_PASS
ROUND = 2
ROUNDS = SAMPLES // ROUND
SCALE_ROWS = 4
QUADRANTS = 4
SUM_SLOT = 8

FLOPS = 2 * SAMPLES * L * E * QD + 2 * SAMPLES * L * QD * QD


SPLIT_SAMPLES = 4
TAIL_SPLIT = False
HEAD = 0
W_AFTER = 1


def tile_parallelretention_pb_kernel(tc, x, Wq_words, Wq_scales, bq, kv, decay_mask, out):
    nc = tc.nc
    with ExitStack() as ctx:
        const = ctx.enter_context(tc.tile_pool(name="const", bufs=1))
        x_pool = ctx.enter_context(tc.tile_pool(name="x", bufs=SAMPLES))
        kv_pool = ctx.enter_context(tc.tile_pool(name="kv", bufs=ROUNDS))
        grouped_pool = ctx.enter_context(tc.tile_pool(name="grouped", bufs=4))
        code_pool = ctx.enter_context(tc.tile_pool(name="codes", bufs=2 * ROUND * BANKS_PER_SAMPLE))
        work = ctx.enter_context(tc.tile_pool(name="work", bufs=4))
        y_pool = ctx.enter_context(tc.tile_pool(name="y", bufs=6))
        res_pool = ctx.enter_context(tc.tile_pool(name="res", bufs=ROUNDS))
        psum_turn = ctx.enter_context(tc.psum_pool(name="psum_turn", bufs=4))
        psum_qg = ctx.enter_context(tc.psum_pool(name="psum_qg", bufs=2))
        psum_small = ctx.enter_context(tc.psum_pool(name="psum_small", bufs=1))
        ctx.enter_context(tc.manual_schedule())

        ident_f32 = const.tile([P, P], F32)
        make_identity(nc, ident_f32[:])
        ident_bf16 = const.tile([P, P], BF16)
        make_identity(nc, ident_bf16[:])
        bias_sheet = const.tile([P, QD], BF16)
        nc.vector.memset(bias_sheet[:], 0.0)
        ones = const.tile([P, P], BF16)
        nc.vector.memset(ones[:], 1.0)
        w_scales = const.tile([P, PASSES, QD], U8, align_bytes=64)
        nc.vector.memset(w_scales[:].bitcast(I32), 0)
        mean_weights = const.tile([P, P], F32)
        nc.vector.memset(mean_weights[:], 1.0 / (L * QD))
        table_seed = const.tile([P, 1], F32)
        nc.vector.memset(table_seed[:], 1.0)

        x_rows = {}
        kv_rows = {}

        def load_x(s):
            x_sample = x_pool.tile([L, E], BF16)
            if s < SPLIT_SAMPLES:
                for b in range(BANKS_PER_SAMPLE):
                    nc.sync.dma_start(
                        out=x_sample[:, b * K_BANK : (b + 1) * K_BANK], in_=x[s, 0, :, b * K_BANK : (b + 1) * K_BANK]
                    )
            else:
                nc.sync.dma_start(out=x_sample[:], in_=x[s, 0, :, :])
            for b in range(BANKS_PER_SAMPLE):
                x_rows[(s, b)] = x_sample[:, b * K_BANK : (b + 1) * K_BANK]

        def load_kv(r, queue):
            kv_round = kv_pool.tile([L, ROUND, QD], BF16)
            queue.dma_start(
                out=kv_round[:], in_=kv[r * ROUND : (r + 1) * ROUND, 0, :, :].rearrange("s l k -> l s k")
            )
            kv_rows[r] = kv_round

        decay_rows = const.tile([QD, QD], BF16)
        w_words = const.tile([P, PASSES, 2 * QD], U8, align_bytes=64)

        def load_small(queue):
            queue.dma_start(out=decay_rows[:], in_=decay_mask[0, :, :])
            load_kv(0, queue)
            queue.dma_start(out=bias_sheet[0:1, :], in_=bq.unsqueeze(0))

        def load_w():
            nc.sync.dma_start(out=w_words[:].bitcast(I32), in_=Wq_words.bitcast(I32).rearrange("g p w -> p g w"))
            for quad in range(QUADRANTS):
                nc.sync.dma_start(
                    out=w_scales[32 * quad : 32 * quad + SCALE_ROWS, :, :].bitcast(I32),
                    in_=Wq_scales.bitcast(I32)[:, SCALE_ROWS * quad : SCALE_ROWS * (quad + 1), :].rearrange(
                        "g r w -> r g w"
                    ),
                )

        if HEAD == 0:
            load_small(nc.scalar)
        nc.scalar.activation(out=table_seed[:], in_=table_seed[:], func=ACT.Abs_reciprocal_sqrt)
        for r in range(ROUNDS):
            for j in range(ROUND):
                load_x(r * ROUND + j)
            if r == 0 and HEAD == 1:
                load_small(nc.sync)
            if r > 0:
                load_kv(r, nc.sync)
            if r + 1 == W_AFTER:
                load_w()

        groups = {}
        codes = {}
        planes = {}
        kv_turned = {}
        q_banks = {}
        g_banks = {}
        biased = {}
        products = {}
        sums = {}
        moments = {}
        means = {}
        spreads = {}
        inverses = {}
        results = {}
        last_round = ROUNDS - 1
        both = tuple(range(ROUND))

        PAIRED = ROUNDS - 2

        def group(r):
            return r // 2 if r < PAIRED else r - PAIRED // 2

        def closes_group(r):
            return r >= PAIRED or r % 2 == 1

        def width(r):
            return 2 * ROUND if r < PAIRED else ROUND

        def col(r, j):
            return (r % 2) * ROUND + j if r < PAIRED else j

        def split(r):
            return TAIL_SPLIT and r == last_round

        def live(r):
            return 0 <= r < ROUNDS

        def turn_x(r, j, b):
            x_words = x_rows[(r * ROUND + j, b)].bitcast(F32)
            turned = psum_turn.tile([P, TURNS_PER_BANK, L], F32)
            for i in range(PASSES_PER_BANK):
                first = i * (K_PASS // 2)
                for u in range(PAIRS):
                    nc.tensor.transpose(
                        turned[:, i * PAIRS + u, :],
                        x_words[:, first + u : first + K_PASS // 2 : PAIRS],
                        ident_f32[:],
                    )
            grouped = grouped_pool.tile([P, PASSES_PER_BANK * L * PACK], BF16, align_bytes=64)
            nc.scalar.copy(
                out=grouped[:].bitcast(F32).rearrange("p (i l u) -> p i l u", i=PASSES_PER_BANK, u=PAIRS),
                in_=turned[:].rearrange("p (i u) l -> p i l u", u=PAIRS),
            )
            groups[(r, j, b)] = grouped

        def quantise_x(r, j, b):
            x_codes = code_pool.tile([P, PASSES_PER_BANK * L], U32, align_bytes=64)
            x_scales = code_pool.tile([P, PASSES_PER_BANK * L], U8, align_bytes=64)
            nc.vector.quantize_mx(out=x_codes[:].bitcast(FP8X4), scales=x_scales[:], in_=groups[(r, j, b)][:])
            codes[(r, j, b)] = x_codes
            planes[(r, j, b)] = x_scales

        def turn_kv(r):
            kv_bank = psum_small.tile([QD, ROUND, L], BF16)
            for j in range(ROUND):
                nc.tensor.transpose(kv_bank[:, j, :], kv_rows[r][:, j, :], ident_bf16[:])
            kv_cols = work.tile([QD, ROUND, L], BF16)
            nc.vector.tensor_copy(out=kv_cols[:], in_=kv_bank[:])
            kv_turned[r] = kv_cols

        def multiply(r):
            if split(r):
                for j in both:
                    own = psum_turn.tile([L, 2 * ROUND, QD], F32, tag="turned")
                    q_banks[(r, j)] = own[:, 0, :]
                    g_banks[(r, j)] = own[:, 1, :]
            else:
                qg = psum_qg.tile([L, 2 * ROUND, QD], F32)
                for j in both:
                    q_banks[(r, j)] = qg[:, j, :]
                    g_banks[(r, j)] = qg[:, ROUND + j, :]
                q_banks[r] = qg[:, 0:ROUND, :]
            g_last = live(r + 2)

            def plain():
                for j in both:
                    nc.tensor.matmul(
                        out=g_banks[(r, j)], lhsT=kv_turned[r][:, j, :], rhs=decay_turned[:], start=True, stop=True
                    )

            if not g_last:
                plain()
            for j in both:
                for g in range(PASSES):
                    b, i = divmod(g, PASSES_PER_BANK)
                    rows = slice(i * L, (i + 1) * L)
                    nc.tensor.matmul_mx(
                        out=q_banks[(r, j)],
                        lhsT=codes[(r, j, b)][:, rows].bitcast(FP8X4),
                        lhsT_scale=planes[(r, j, b)][:, rows],
                        rhs=w_words[:, g, :].bitcast(FP4X4),
                        rhs_scale=w_scales[:, g, :],
                        start=(g == 0),
                        stop=(g == PASSES - 1),
                    )
            if g_last:
                plain()

        def add_bias(r, js):
            if r not in biased:
                q_biased = work.tile([L, ROUND, QD], F32)
                biased[r] = q_biased
            if js == both:
                nc.vector.tensor_tensor(
                    out=biased[r][:],
                    in0=q_banks[r],
                    in1=bias_rows[:].unsqueeze(1).to_broadcast([L, ROUND, QD]),
                    op=ALU.add,
                )
            else:
                for j in js:
                    nc.vector.tensor_tensor(out=biased[r][:, j, :], in0=q_banks[(r, j)], in1=bias_rows[:], op=ALU.add)

        def product(r, js):
            if r not in products:
                y = y_pool.tile([L, ROUND, QD], F32)
                products[r] = y
            if group(r) not in sums:
                row_sums = work.tile([L, 2, SUM_SLOT], F32)
                sums[group(r)] = row_sums
            for j in js:
                nc.vector.scalar_tensor_tensor(
                    out=products[r][:, j, :],
                    in0=biased[r][:, j, :],
                    scalar=1.0,
                    in1=g_banks[(r, j)],
                    op0=ALU.mult,
                    op1=ALU.mult,
                    accum_out=sums[group(r)][:, 0, col(r, j) : col(r, j) + 1],
                )

        def square(r, js):
            for j in js:
                squares = work.tile([L, QD], F32)
                nc.scalar.activation(
                    out=squares[:],
                    in_=products[r][:, j, :],
                    func=ACT.Square,
                    accum_out=sums[group(r)][:, 1, col(r, j) : col(r, j) + 1],
                )

        def average(r):
            moment_bank = psum_small.tile([P, 2, width(r)], F32)
            nc.tensor.matmul(
                out=moment_bank[:], lhsT=mean_weights[:], rhs=sums[group(r)][:, :, 0 : width(r)], start=True, stop=True
            )
            moments[group(r)] = moment_bank

        def spread(r):
            minus_var = work.tile([P, width(r)], F32)
            bank = moments[group(r)]
            for c in range(width(r)):
                nc.vector.tensor_scalar(
                    out=minus_var[:, c : c + 1],
                    in0=bank[:, 0, c : c + 1],
                    scalar1=bank[:, 0, c : c + 1],
                    scalar2=bank[:, 1, c : c + 1],
                    op0=ALU.mult,
                    op1=ALU.subtract,
                )
            mean = work.tile([P, width(r)], F32)
            nc.vector.tensor_copy(out=mean[:], in_=bank[:, 0, :])
            means[group(r)] = mean
            spreads[group(r)] = minus_var

        def inverse_deviation(r):
            inverse = work.tile([P, width(r)], F32)
            nc.scalar.activation(
                out=inverse[:], in_=spreads[group(r)][:], func=ACT.Abs_reciprocal_sqrt, scale=-1.0, bias=EPS
            )
            inverses[group(r)] = inverse

        def normalise(r):
            res = res_pool.tile([L, ROUND, QD], F32)
            for j in both:
                c = col(r, j)
                nc.vector.tensor_scalar(
                    out=res[:, j, :],
                    in0=products[r][:, j, :],
                    scalar1=means[group(r)][:, c : c + 1],
                    scalar2=inverses[group(r)][:, c : c + 1],
                    op0=ALU.subtract,
                    op1=ALU.mult,
                )
            nc.sync.dma_start(out=out[r * ROUND : (r + 1) * ROUND, :, :].rearrange("s l q -> l s q"), in_=res[:])

        def make_constants():
            decay_bank = psum_small.tile([QD, ROUND, QD], BF16, tag="kv_bank")
            nc.tensor.transpose(decay_bank[:, 0, :], decay_rows[:], ident_bf16[:])
            nc.vector.tensor_copy(out=decay_turned[:], in_=decay_bank[:, 0, :])
            bias_bank = psum_small.tile([P, QD], F32, tag="moment_bank")
            nc.tensor.matmul(out=bias_bank[:], lhsT=ones[:], rhs=bias_sheet[:], start=True, stop=True)
            nc.vector.tensor_copy(out=bias_rows[:], in_=bias_bank[:])

        decay_turned = const.tile([QD, QD], BF16)
        bias_rows = const.tile([P, QD], F32)
        if HEAD == 0:
            make_constants()

        last = ROUND - 1

        def stats_due(t):
            return live(t - 3) and closes_group(t - 3)

        for t in range(ROUNDS + 4):
            if live(t - 2):
                add_bias(t - 2, both)
                product(t - 2, both)
            for r in (t - 5, t - 4):
                if live(r) and (r < PAIRED) == (r == t - 5):
                    normalise(r)
            if live(t):
                for j in range(last):
                    for b in range(BANKS_PER_SAMPLE):
                        turn_x(t, j, b)
                        quantise_x(t, j, b)
                for b in range(BANKS_PER_SAMPLE):
                    turn_x(t, last, b)
                turn_kv(t)
            if live(t - 1) and not live(t):
                multiply(t - 1)
            if stats_due(t):
                average(t - 3)
                spread(t - 3)
            if live(t):
                for b in range(BANKS_PER_SAMPLE):
                    quantise_x(t, last, b)
            if live(t - 1) and live(t):
                multiply(t - 1)
            if live(t - 2):
                square(t - 2, both)
            if stats_due(t):
                inverse_deviation(t - 3)
